import numpy as np
import ml_dtypes

BF16 = ml_dtypes.bfloat16


def bf(x):
    return np.asarray(x, np.float32).astype(BF16)


def f32(x):
    return np.asarray(x, np.float32)


def f64(x):
    return np.asarray(x).astype(np.float64)


def striped(idx):
    return np.tile(idx.reshape(-1, 16).T, (8, 1))


C, CH, S, N, P, F = 1024, 512, 512, 256, 128, 64
ROPE_BASE = 10000.0


def rope_tables():
    inv = f32(1.0) / f32(ROPE_BASE) ** (f32(np.arange(F)) / f32(F))
    ang = f32(np.arange(N))[None, :] * inv[:, None]
    reps = (P // F, 1)
    return f32(np.tile(np.cos(f64(ang)), reps)), f32(np.tile(np.sin(f64(ang)), reps))


def setup_inputs():
    cos_t, sin_t = rope_tables()
    return {"x": f32(np.random.standard_normal((C, S))), "cos_t": cos_t, "sin_t": sin_t, "offs": striped(np.random.permutation(S)[:N])}


def reference(x, cos_t, sin_t, offs):
    idx = offs[:16].T.reshape(-1)
    xg = f64(x)[:, idx]
    lo, hi = xg[:CH], xg[CH:]
    c = np.tile(f64(cos_t), (CH // P, 1))
    s = np.tile(f64(sin_t), (CH // P, 1))
    return np.concatenate([lo * c - hi * s, hi * c + lo * s], axis=0)

@@ -1,0 +1,54 @@
+import concourse.mybir as mybir
+
+P = 128
+SLOTS = 512
+N = 256
+PAIRS = 4
+
+F32 = mybir.dt.float32
+U16 = mybir.dt.uint16
+MULT = mybir.AluOpType.mult
+
+
+def tile_streamingattentionsink_kernel(tc, x, cos_t, sin_t, offs, out):
+    nc = tc.nc
+    with (
+        tc.tile_pool(name="held", bufs=1) as held,
+        tc.tile_pool(name="work", bufs=PAIRS) as work,
+    ):
+        offsets = held.tile([P, N // 16], U16, name="offsets")
+        nc.sync.dma_start(offsets[:], offs)
+        cos = held.tile([P, N], F32, name="cos")
+        nc.scalar.dma_start(cos[:], cos_t)
+        sin = held.tile([P, N], F32, name="sin")
+        nc.scalar.dma_start(sin[:], sin_t)
+
+        lo_blocks = []
+        hi_blocks = []
+        for b in range(PAIRS):
+            lo = held.tile([P, SLOTS], F32, name=f"lo{b}")
+            nc.sync.dma_start(lo[:], x[b * P : (b + 1) * P, :])
+            lo_blocks.append(lo)
+            hi = held.tile([P, SLOTS], F32, name=f"hi{b}")
+            nc.scalar.dma_start(hi[:], x[(PAIRS + b) * P : (PAIRS + b + 1) * P, :])
+            hi_blocks.append(hi)
+
+        for b in range(PAIRS):
+            lo_picked = lo_blocks[b][:].indirect(offsets[:])
+            hi_picked = hi_blocks[b][:].indirect(offsets[:])
+
+            lo_cos = work.tile([P, N], F32, name="lo_cos")
+            nc.vector.tensor_tensor(lo_cos[:], lo_picked, cos[:], MULT)
+            lo_sin = work.tile([P, N], F32, name="lo_sin")
+            nc.vector.tensor_tensor(lo_sin[:], lo_picked, sin[:], MULT)
+            hi_sin = work.tile([P, N], F32, name="hi_sin")
+            nc.vector.tensor_tensor(hi_sin[:], hi_picked, sin[:], MULT)
+            hi_cos = work.tile([P, N], F32, name="hi_cos")
+            nc.vector.tensor_tensor(hi_cos[:], hi_picked, cos[:], MULT)
+
+            out_lo = work.tile([P, N], F32, name="out_lo")
+            nc.vector.tensor_sub(out_lo[:], lo_cos[:], hi_sin[:])
+            nc.sync.dma_start(out[b * P : (b + 1) * P, :], out_lo[:])
+            out_hi = work.tile([P, N], F32, name="out_hi")
+            nc.vector.tensor_add(out_hi[:], hi_cos[:], lo_sin[:])
+            nc.scalar.dma_start(out[(PAIRS + b) * P : (PAIRS + b + 1) * P, :], out_hi[:])

@@ -1,4 +1,5 @@
 import concourse.mybir as mybir
+from concourse.masks import make_identity
 
 P = 128
 SLOTS = 512
@@ -15,6 +16,7 @@ def tile_streamingattentionsink_kernel(tc, x, cos_t, sin_t, offs, out):
     with (
         tc.tile_pool(name="held", bufs=1) as held,
         tc.tile_pool(name="work", bufs=PAIRS) as work,
+        tc.psum_pool(name="sums", bufs=PAIRS) as sums,
     ):
         offsets = held.tile([P, N // 16], U16, name="offsets")
         nc.sync.dma_start(offsets[:], offs)
@@ -33,22 +35,33 @@ def tile_streamingattentionsink_kernel(tc, x, cos_t, sin_t, offs, out):
             nc.scalar.dma_start(hi[:], x[(PAIRS + b) * P : (PAIRS + b + 1) * P, :])
             hi_blocks.append(hi)
 
+        identity = held.tile([P, P], F32, name="identity")
+        make_identity(nc, identity[:])
+        neg_sin = held.tile([P, N], F32, name="neg_sin")
+        nc.scalar.mul(neg_sin[:], sin[:], -1.0)
+
         for b in range(PAIRS):
             lo_picked = lo_blocks[b][:].indirect(offsets[:])
             hi_picked = hi_blocks[b][:].indirect(offsets[:])
+            sum_lo = sums.tile([P, N], F32, name="sum_lo")
+            sum_hi = sums.tile([P, N], F32, name="sum_hi")
 
             lo_cos = work.tile([P, N], F32, name="lo_cos")
             nc.vector.tensor_tensor(lo_cos[:], lo_picked, cos[:], MULT)
+            nc.tensor.matmul(sum_lo[:], identity[:], lo_cos[:], start=True, stop=False)
             lo_sin = work.tile([P, N], F32, name="lo_sin")
             nc.vector.tensor_tensor(lo_sin[:], lo_picked, sin[:], MULT)
-            hi_sin = work.tile([P, N], F32, name="hi_sin")
-            nc.vector.tensor_tensor(hi_sin[:], hi_picked, sin[:], MULT)
+            nc.tensor.matmul(sum_hi[:], identity[:], lo_sin[:], start=True, stop=False)
+            hi_neg_sin = work.tile([P, N], F32, name="hi_neg_sin")
+            nc.vector.tensor_tensor(hi_neg_sin[:], hi_picked, neg_sin[:], MULT)
+            nc.tensor.matmul(sum_lo[:], identity[:], hi_neg_sin[:], start=False, stop=True)
             hi_cos = work.tile([P, N], F32, name="hi_cos")
             nc.vector.tensor_tensor(hi_cos[:], hi_picked, cos[:], MULT)
+            nc.tensor.matmul(sum_hi[:], identity[:], hi_cos[:], start=False, stop=True)
 
             out_lo = work.tile([P, N], F32, name="out_lo")
-            nc.vector.tensor_sub(out_lo[:], lo_cos[:], hi_sin[:])
+            nc.scalar.copy(out_lo[:], sum_lo[:])
             nc.sync.dma_start(out[b * P : (b + 1) * P, :], out_lo[:])
             out_hi = work.tile([P, N], F32, name="out_hi")
-            nc.vector.tensor_add(out_hi[:], hi_cos[:], lo_sin[:])
-            nc.scalar.dma_start(out[(PAIRS + b) * P : (PAIRS + b + 1) * P, :], out_hi[:])
+            nc.scalar.copy(out_hi[:], sum_hi[:])
+            nc.sync.dma_start(out[(PAIRS + b) * P : (PAIRS + b + 1) * P, :], out_hi[:])

@@ -16,52 +16,57 @@ def tile_streamingattentionsink_kernel(tc, x, cos_t, sin_t, offs, out):
     with (
         tc.tile_pool(name="held", bufs=1) as held,
         tc.tile_pool(name="work", bufs=PAIRS) as work,
-        tc.psum_pool(name="sums", bufs=PAIRS) as sums,
+        tc.psum_pool(name="sums", bufs=PAIRS - 1) as sums,
     ):
         offsets = held.tile([P, N // 16], U16, name="offsets")
         nc.sync.dma_start(offsets[:], offs)
         cos = held.tile([P, N], F32, name="cos")
-        nc.scalar.dma_start(cos[:], cos_t)
         sin = held.tile([P, N], F32, name="sin")
-        nc.scalar.dma_start(sin[:], sin_t)
-
-        lo_blocks = []
-        hi_blocks = []
-        for b in range(PAIRS):
-            lo = held.tile([P, SLOTS], F32, name=f"lo{b}")
-            nc.sync.dma_start(lo[:], x[b * P : (b + 1) * P, :])
-            lo_blocks.append(lo)
-            hi = held.tile([P, SLOTS], F32, name=f"hi{b}")
-            nc.scalar.dma_start(hi[:], x[(PAIRS + b) * P : (PAIRS + b + 1) * P, :])
-            hi_blocks.append(hi)
+        lo_blocks = [held.tile([P, SLOTS], F32, name=f"lo{b}") for b in range(PAIRS)]
+        hi_blocks = [held.tile([P, SLOTS], F32, name=f"hi{b}") for b in range(PAIRS)]
+        nc.sync.dma_start(lo_blocks[0][:], x[0:P, :])
+        nc.sync.dma_start(cos[:], cos_t)
+        nc.sync.dma_start(sin[:], sin_t)
+        nc.sync.dma_start(hi_blocks[0][:], x[PAIRS * P : (PAIRS + 1) * P, :])
+        for b in range(1, PAIRS):
+            nc.sync.dma_start(lo_blocks[b][:], x[b * P : (b + 1) * P, :])
+            nc.sync.dma_start(hi_blocks[b][:], x[(PAIRS + b) * P : (PAIRS + b + 1) * P, :])
 
         identity = held.tile([P, P], F32, name="identity")
         make_identity(nc, identity[:])
-        neg_sin = held.tile([P, N], F32, name="neg_sin")
-        nc.scalar.mul(neg_sin[:], sin[:], -1.0)
+        neg_identity = held.tile([P, P], F32, name="neg_identity")
+        nc.gpsimd.tensor_scalar_mul(neg_identity[:], identity[:], -1.0)
 
         for b in range(PAIRS):
             lo_picked = lo_blocks[b][:].indirect(offsets[:])
             hi_picked = hi_blocks[b][:].indirect(offsets[:])
-            sum_lo = sums.tile([P, N], F32, name="sum_lo")
-            sum_hi = sums.tile([P, N], F32, name="sum_hi")
+            lo_rows = out[b * P : (b + 1) * P, :]
+            hi_rows = out[(PAIRS + b) * P : (PAIRS + b + 1) * P, :]
 
             lo_cos = work.tile([P, N], F32, name="lo_cos")
             nc.vector.tensor_tensor(lo_cos[:], lo_picked, cos[:], MULT)
-            nc.tensor.matmul(sum_lo[:], identity[:], lo_cos[:], start=True, stop=False)
             lo_sin = work.tile([P, N], F32, name="lo_sin")
             nc.vector.tensor_tensor(lo_sin[:], lo_picked, sin[:], MULT)
-            nc.tensor.matmul(sum_hi[:], identity[:], lo_sin[:], start=True, stop=False)
-            hi_neg_sin = work.tile([P, N], F32, name="hi_neg_sin")
-            nc.vector.tensor_tensor(hi_neg_sin[:], hi_picked, neg_sin[:], MULT)
-            nc.tensor.matmul(sum_lo[:], identity[:], hi_neg_sin[:], start=False, stop=True)
+            hi_sin = work.tile([P, N], F32, name="hi_sin")
+            nc.vector.tensor_tensor(hi_sin[:], hi_picked, sin[:], MULT)
             hi_cos = work.tile([P, N], F32, name="hi_cos")
             nc.vector.tensor_tensor(hi_cos[:], hi_picked, cos[:], MULT)
-            nc.tensor.matmul(sum_hi[:], identity[:], hi_cos[:], start=False, stop=True)
 
             out_lo = work.tile([P, N], F32, name="out_lo")
-            nc.scalar.copy(out_lo[:], sum_lo[:])
-            nc.sync.dma_start(out[b * P : (b + 1) * P, :], out_lo[:])
             out_hi = work.tile([P, N], F32, name="out_hi")
-            nc.scalar.copy(out_hi[:], sum_hi[:])
-            nc.sync.dma_start(out[(PAIRS + b) * P : (PAIRS + b + 1) * P, :], out_hi[:])
+            if b < PAIRS - 1:
+                difference = sums.tile([P, N], F32, name="difference")
+                total = sums.tile([P, N], F32, name="total")
+                nc.tensor.matmul(difference[:], identity[:], lo_cos[:], start=True, stop=False)
+                nc.tensor.matmul(total[:], identity[:], lo_sin[:], start=True, stop=False)
+                nc.tensor.matmul(difference[:], neg_identity[:], hi_sin[:], start=False, stop=True)
+                nc.tensor.matmul(total[:], identity[:], hi_cos[:], start=False, stop=True)
+                nc.scalar.copy(out_lo[:], difference[:])
+                nc.scalar.dma_start(lo_rows, out_lo[:])
+                nc.scalar.copy(out_hi[:], total[:])
+                nc.scalar.dma_start(hi_rows, out_hi[:])
+            else:
+                nc.vector.tensor_sub(out_lo[:], lo_cos[:], hi_sin[:])
+                nc.sync.dma_start(lo_rows, out_lo[:])
+                nc.vector.tensor_add(out_hi[:], hi_cos[:], lo_sin[:])
+                nc.sync.dma_start(hi_rows, out_hi[:])

@@ -19,13 +19,13 @@ def tile_streamingattentionsink_kernel(tc, x, cos_t, sin_t, offs, out):
         tc.psum_pool(name="sums", bufs=PAIRS - 1) as sums,
     ):
         offsets = held.tile([P, N // 16], U16, name="offsets")
-        nc.sync.dma_start(offsets[:], offs)
         cos = held.tile([P, N], F32, name="cos")
         sin = held.tile([P, N], F32, name="sin")
         lo_blocks = [held.tile([P, SLOTS], F32, name=f"lo{b}") for b in range(PAIRS)]
         hi_blocks = [held.tile([P, SLOTS], F32, name=f"hi{b}") for b in range(PAIRS)]
         nc.sync.dma_start(lo_blocks[0][:], x[0:P, :])
         nc.sync.dma_start(cos[:], cos_t)
+        nc.sync.dma_start(offsets[:], offs)
         nc.sync.dma_start(sin[:], sin_t)
         nc.sync.dma_start(hi_blocks[0][:], x[PAIRS * P : (PAIRS + 1) * P, :])
         for b in range(1, PAIRS):

@@ -4,6 +4,7 @@ from concourse.masks import make_identity
 P = 128
 SLOTS = 512
 N = 256
+HALF = N // 2
 PAIRS = 4
 
 F32 = mybir.dt.float32
@@ -24,8 +25,9 @@ def tile_streamingattentionsink_kernel(tc, x, cos_t, sin_t, offs, out):
         lo_blocks = [held.tile([P, SLOTS], F32, name=f"lo{b}") for b in range(PAIRS)]
         hi_blocks = [held.tile([P, SLOTS], F32, name=f"hi{b}") for b in range(PAIRS)]
         nc.sync.dma_start(lo_blocks[0][:], x[0:P, :])
-        nc.sync.dma_start(cos[:], cos_t)
+        nc.sync.dma_start(cos[:, 0:HALF], cos_t[:, 0:HALF])
         nc.sync.dma_start(offsets[:], offs)
+        nc.sync.dma_start(cos[:, HALF:N], cos_t[:, HALF:N])
         nc.sync.dma_start(sin[:], sin_t)
         nc.sync.dma_start(hi_blocks[0][:], x[PAIRS * P : (PAIRS + 1) * P, :])
         for b in range(1, PAIRS):
@@ -44,7 +46,14 @@ def tile_streamingattentionsink_kernel(tc, x, cos_t, sin_t, offs, out):
             hi_rows = out[(PAIRS + b) * P : (PAIRS + b + 1) * P, :]
 
             lo_cos = work.tile([P, N], F32, name="lo_cos")
-            nc.vector.tensor_tensor(lo_cos[:], lo_picked, cos[:], MULT)
+            if b == 0:
+                for start in (0, HALF):
+                    piece = lo_blocks[b][:].indirect(offsets[:, start // 16 : (start + HALF) // 16])
+                    nc.vector.tensor_tensor(
+                        lo_cos[:, start : start + HALF], piece, cos[:, start : start + HALF], MULT
+                    )
+            else:
+                nc.vector.tensor_tensor(lo_cos[:], lo_picked, cos[:], MULT)
             lo_sin = work.tile([P, N], F32, name="lo_sin")
             nc.vector.tensor_tensor(lo_sin[:], lo_picked, sin[:], MULT)
             hi_sin = work.tile([P, N], F32, name="hi_sin")

@@ -4,7 +4,7 @@ from concourse.masks import make_identity
 P = 128
 SLOTS = 512
 N = 256
-HALF = N // 2
+FIRST = 64
 PAIRS = 4
 
 F32 = mybir.dt.float32
@@ -25,9 +25,9 @@ def tile_streamingattentionsink_kernel(tc, x, cos_t, sin_t, offs, out):
         lo_blocks = [held.tile([P, SLOTS], F32, name=f"lo{b}") for b in range(PAIRS)]
         hi_blocks = [held.tile([P, SLOTS], F32, name=f"hi{b}") for b in range(PAIRS)]
         nc.sync.dma_start(lo_blocks[0][:], x[0:P, :])
-        nc.sync.dma_start(cos[:, 0:HALF], cos_t[:, 0:HALF])
+        nc.sync.dma_start(cos[:, 0:FIRST], cos_t[:, 0:FIRST])
         nc.sync.dma_start(offsets[:], offs)
-        nc.sync.dma_start(cos[:, HALF:N], cos_t[:, HALF:N])
+        nc.sync.dma_start(cos[:, FIRST:N], cos_t[:, FIRST:N])
         nc.sync.dma_start(sin[:], sin_t)
         nc.sync.dma_start(hi_blocks[0][:], x[PAIRS * P : (PAIRS + 1) * P, :])
         for b in range(1, PAIRS):
@@ -47,11 +47,9 @@ def tile_streamingattentionsink_kernel(tc, x, cos_t, sin_t, offs, out):
 
             lo_cos = work.tile([P, N], F32, name="lo_cos")
             if b == 0:
-                for start in (0, HALF):
-                    piece = lo_blocks[b][:].indirect(offsets[:, start // 16 : (start + HALF) // 16])
-                    nc.vector.tensor_tensor(
-                        lo_cos[:, start : start + HALF], piece, cos[:, start : start + HALF], MULT
-                    )
+                for start, stop in ((0, FIRST), (FIRST, N)):
+                    piece = lo_blocks[b][:].indirect(offsets[:, start // 16 : stop // 16])
+                    nc.vector.tensor_tensor(lo_cos[:, start:stop], piece, cos[:, start:stop], MULT)
             else:
                 nc.vector.tensor_tensor(lo_cos[:], lo_picked, cos[:], MULT)
             lo_sin = work.tile([P, N], F32, name="lo_sin")

@@ -69,9 +69,9 @@ def tile_streamingattentionsink_kernel(tc, x, cos_t, sin_t, offs, out):
                 nc.tensor.matmul(difference[:], neg_identity[:], hi_sin[:], start=False, stop=True)
                 nc.tensor.matmul(total[:], identity[:], hi_cos[:], start=False, stop=True)
                 nc.scalar.copy(out_lo[:], difference[:])
-                nc.scalar.dma_start(lo_rows, out_lo[:])
+                nc.sync.dma_start(lo_rows, out_lo[:])
                 nc.scalar.copy(out_hi[:], total[:])
-                nc.scalar.dma_start(hi_rows, out_hi[:])
+                nc.sync.dma_start(hi_rows, out_hi[:])
             else:
                 nc.vector.tensor_sub(out_lo[:], lo_cos[:], hi_sin[:])
                 nc.sync.dma_start(lo_rows, out_lo[:])

@@ -39,11 +39,10 @@ def tile_streamingattentionsink_kernel(tc, x, cos_t, sin_t, offs, out):
         neg_identity = held.tile([P, P], F32, name="neg_identity")
         nc.gpsimd.tensor_scalar_mul(neg_identity[:], identity[:], -1.0)
 
+        out_pairs = out.rearrange("(h b p) n -> p b h n", h=2, p=P)
         for b in range(PAIRS):
             lo_picked = lo_blocks[b][:].indirect(offsets[:])
             hi_picked = hi_blocks[b][:].indirect(offsets[:])
-            lo_rows = out[b * P : (b + 1) * P, :]
-            hi_rows = out[(PAIRS + b) * P : (PAIRS + b + 1) * P, :]
 
             lo_cos = work.tile([P, N], F32, name="lo_cos")
             if b == 0:
@@ -59,21 +58,21 @@ def tile_streamingattentionsink_kernel(tc, x, cos_t, sin_t, offs, out):
             hi_cos = work.tile([P, N], F32, name="hi_cos")
             nc.vector.tensor_tensor(hi_cos[:], hi_picked, cos[:], MULT)
 
-            out_lo = work.tile([P, N], F32, name="out_lo")
-            out_hi = work.tile([P, N], F32, name="out_hi")
             if b < PAIRS - 1:
+                both = work.tile([P, 2, N], F32, name="both")
                 difference = sums.tile([P, N], F32, name="difference")
                 total = sums.tile([P, N], F32, name="total")
                 nc.tensor.matmul(difference[:], identity[:], lo_cos[:], start=True, stop=False)
                 nc.tensor.matmul(total[:], identity[:], lo_sin[:], start=True, stop=False)
                 nc.tensor.matmul(difference[:], neg_identity[:], hi_sin[:], start=False, stop=True)
                 nc.tensor.matmul(total[:], identity[:], hi_cos[:], start=False, stop=True)
-                nc.scalar.copy(out_lo[:], difference[:])
-                nc.sync.dma_start(lo_rows, out_lo[:])
-                nc.scalar.copy(out_hi[:], total[:])
-                nc.sync.dma_start(hi_rows, out_hi[:])
+                nc.scalar.copy(both[:, 0, :], difference[:])
+                nc.scalar.copy(both[:, 1, :], total[:])
+                nc.scalar.dma_start(out_pairs[:, b, :, :], both[:])
             else:
+                out_lo = work.tile([P, N], F32, name="out_lo")
+                out_hi = work.tile([P, N], F32, name="out_hi")
                 nc.vector.tensor_sub(out_lo[:], lo_cos[:], hi_sin[:])
-                nc.sync.dma_start(lo_rows, out_lo[:])
+                nc.sync.dma_start(out_pairs[:, b, 0, :], out_lo[:])
                 nc.vector.tensor_add(out_hi[:], hi_cos[:], lo_sin[:])
-                nc.sync.dma_start(hi_rows, out_hi[:])
+                nc.sync.dma_start(out_pairs[:, b, 1, :], out_hi[:])

@@ -67,8 +67,13 @@ def tile_streamingattentionsink_kernel(tc, x, cos_t, sin_t, offs, out):
                 nc.tensor.matmul(difference[:], neg_identity[:], hi_sin[:], start=False, stop=True)
                 nc.tensor.matmul(total[:], identity[:], hi_cos[:], start=False, stop=True)
                 nc.scalar.copy(both[:, 0, :], difference[:])
+                if b == PAIRS - 2:
+                    nc.scalar.dma_start(out_pairs[:, b, 0, :], both[:, 0, :])
                 nc.scalar.copy(both[:, 1, :], total[:])
-                nc.scalar.dma_start(out_pairs[:, b, :, :], both[:])
+                if b == PAIRS - 2:
+                    nc.scalar.dma_start(out_pairs[:, b, 1, :], both[:, 1, :])
+                else:
+                    nc.scalar.dma_start(out_pairs[:, b, :, :], both[:])
             else:
                 out_lo = work.tile([P, N], F32, name="out_lo")
                 out_hi = work.tile([P, N], F32, name="out_hi")

import concourse.mybir as mybir
from concourse.masks import make_identity

P = 128
SLOTS = 512
N = 256
FIRST = 64
PAIRS = 4

F32 = mybir.dt.float32
U16 = mybir.dt.uint16
MULT = mybir.AluOpType.mult


def tile_streamingattentionsink_kernel(tc, x, cos_t, sin_t, offs, out):
    nc = tc.nc
    with (
        tc.tile_pool(name="held", bufs=1) as held,
        tc.tile_pool(name="work", bufs=PAIRS) as work,
        tc.psum_pool(name="sums", bufs=PAIRS - 1) as sums,
    ):
        offsets = held.tile([P, N // 16], U16, name="offsets")
        cos = held.tile([P, N], F32, name="cos")
        sin = held.tile([P, N], F32, name="sin")
        lo_blocks = [held.tile([P, SLOTS], F32, name=f"lo{b}") for b in range(PAIRS)]
        hi_blocks = [held.tile([P, SLOTS], F32, name=f"hi{b}") for b in range(PAIRS)]
        nc.sync.dma_start(lo_blocks[0][:], x[0:P, :])
        nc.sync.dma_start(cos[:, 0:FIRST], cos_t[:, 0:FIRST])
        nc.sync.dma_start(offsets[:], offs)
        nc.sync.dma_start(cos[:, FIRST:N], cos_t[:, FIRST:N])
        nc.sync.dma_start(sin[:], sin_t)
        nc.sync.dma_start(hi_blocks[0][:], x[PAIRS * P : (PAIRS + 1) * P, :])
        for b in range(1, PAIRS):
            nc.sync.dma_start(lo_blocks[b][:], x[b * P : (b + 1) * P, :])
            nc.sync.dma_start(hi_blocks[b][:], x[(PAIRS + b) * P : (PAIRS + b + 1) * P, :])

        identity = held.tile([P, P], F32, name="identity")
        make_identity(nc, identity[:])
        neg_identity = held.tile([P, P], F32, name="neg_identity")
        nc.gpsimd.tensor_scalar_mul(neg_identity[:], identity[:], -1.0)

        out_pairs = out.rearrange("(h b p) n -> p b h n", h=2, p=P)
        for b in range(PAIRS):
            lo_picked = lo_blocks[b][:].indirect(offsets[:])
            hi_picked = hi_blocks[b][:].indirect(offsets[:])

            lo_cos = work.tile([P, N], F32, name="lo_cos")
            if b == 0:
                for start, stop in ((0, FIRST), (FIRST, N)):
                    piece = lo_blocks[b][:].indirect(offsets[:, start // 16 : stop // 16])
                    nc.vector.tensor_tensor(lo_cos[:, start:stop], piece, cos[:, start:stop], MULT)
            else:
                nc.vector.tensor_tensor(lo_cos[:], lo_picked, cos[:], MULT)
            lo_sin = work.tile([P, N], F32, name="lo_sin")
            nc.vector.tensor_tensor(lo_sin[:], lo_picked, sin[:], MULT)
            hi_sin = work.tile([P, N], F32, name="hi_sin")
            nc.vector.tensor_tensor(hi_sin[:], hi_picked, sin[:], MULT)
            hi_cos = work.tile([P, N], F32, name="hi_cos")
            nc.vector.tensor_tensor(hi_cos[:], hi_picked, cos[:], MULT)

            if b < PAIRS - 1:
                both = work.tile([P, 2, N], F32, name="both")
                difference = sums.tile([P, N], F32, name="difference")
                total = sums.tile([P, N], F32, name="total")
                nc.tensor.matmul(difference[:], identity[:], lo_cos[:], start=True, stop=False)
                nc.tensor.matmul(total[:], identity[:], lo_sin[:], start=True, stop=False)
                nc.tensor.matmul(difference[:], neg_identity[:], hi_sin[:], start=False, stop=True)
                nc.tensor.matmul(total[:], identity[:], hi_cos[:], start=False, stop=True)
                nc.scalar.copy(both[:, 0, :], difference[:])
                if b == PAIRS - 2:
                    nc.scalar.dma_start(out_pairs[:, b, 0, :], both[:, 0, :])
                nc.scalar.copy(both[:, 1, :], total[:])
                if b == PAIRS - 2:
                    nc.scalar.dma_start(out_pairs[:, b, 1, :], both[:, 1, :])
                else:
                    nc.scalar.dma_start(out_pairs[:, b, :, :], both[:])
            else:
                out_lo = work.tile([P, N], F32, name="out_lo")
                out_hi = work.tile([P, N], F32, name="out_hi")
                nc.vector.tensor_sub(out_lo[:], lo_cos[:], hi_sin[:])
                nc.sync.dma_start(out_pairs[:, b, 0, :], out_lo[:])
                nc.vector.tensor_add(out_hi[:], hi_cos[:], lo_sin[:])
                nc.sync.dma_start(out_pairs[:, b, 1, :], out_hi[:])
